import numpy as np
import ml_dtypes


def mxq(x, axis, fmt="e4m3"):
    dtype, down = {"e4m3": (ml_dtypes.float8_e4m3fn, 7), "e5m2": (ml_dtypes.float8_e5m2, 14)}[fmt]
    v = np.moveaxis(np.asarray(x, np.float32).astype(ml_dtypes.bfloat16).astype(np.float64), axis, -1)
    blocks = v.reshape(v.shape[:-1] + (-1, 32))
    amax = np.abs(blocks).max(-1, keepdims=True)
    byte = np.maximum(np.where(amax > 0, np.frexp(amax)[1] - 1 + 127, 0) - down, 1)
    scale = np.exp2(byte - 127.0)
    codes = (blocks / scale).astype(np.float32).astype(dtype).astype(np.float64)
    return np.moveaxis((codes * scale).reshape(v.shape), -1, axis)


WIDE = False


def mx_kscale(k):
    if not WIDE:
        return np.ones(k)
    levels = np.array([10, -10, 5, -5, 0])
    if k % 512:
        return np.exp2(np.random.permutation(np.resize(levels, k // 32))).repeat(32)
    a = np.empty((k // 512, 16))
    for p in range(k // 512):
        a[p, :8] = np.random.permutation(np.resize(levels, 8))
        for g in range(8):
            far = levels[np.abs(levels - a[p, g]) >= 10]
            a[p, g + 8] = far[np.random.randint(len(far))]
    return np.exp2(a.ravel()).repeat(32)


BF16 = ml_dtypes.bfloat16


def bf(x):
    return np.asarray(x, np.float32).astype(BF16)


def f64(x):
    return np.asarray(x).astype(np.float64)


B, L, D, H, HD, FF = 4, 1024, 1024, 2, 128, 4096
EPS = 1e-6
DA = H * HD


def rmsnorm(x, w):
    return x * (1.0 / np.sqrt(np.mean(x * x, axis=-1, keepdims=True) + EPS)) * w


def setup_inputs():
    s = mx_kscale(D)
    return {"x": bf(np.random.standard_normal((B, L, D))),
            "norm1_w": bf((1.0 + 0.1 * np.random.standard_normal(D)) * s),
            "qkv_w": bf(np.random.standard_normal((3 * DA, D)) / np.sqrt(D) / s[None, :])}


def reference(x, norm1_w, qkv_w):
    h = rmsnorm(f64(x), f64(norm1_w))
    qkv = mxq(h, 2, "e4m3") @ mxq(f64(qkv_w), 1, "e4m3").T
    qkv = qkv.reshape(B, L, 3, H, HD)
    q, k, v = (np.moveaxis(qkv, 2, 0)[i].transpose(0, 2, 1, 3) for i in range(3))
    return q, k, v

@@ -1,0 +1,319 @@
+from contextlib import ExitStack
+
+import concourse.mybir as mybir
+from concourse.masks import make_identity
+
+BF16 = mybir.dt.bfloat16
+F32 = mybir.dt.float32
+U32 = mybir.dt.uint32
+U8 = mybir.dt.uint8
+FP8X4 = mybir.dt.float8_e4m3fn_x4
+ACT = mybir.ActivationFunctionType
+ALU = mybir.AluOpType
+
+P = 128
+NB = 4
+L = 1024
+D = 1024
+NOUT = 768
+JB = L // P
+NT = NB * JB
+NP = NT // 2
+EPS = 1e-6
+FLOPS = 2 * NB * L * D * NOUT
+
+PA = 3
+PI = 2
+FB_V_UNTIL = 24
+
+
+def tile_transformerblock_pa_t_kernel(tc, x, norm1_w, qkv_w, out_0, out_1, out_2):
+    nc = tc.nc
+    outs = (out_0, out_1, out_2)
+    xf = x.flatten_outer_dims()
+
+    loads = [(0, 0, 1), (0, 1, 2), (0, 2, 4), (0, 4, 8)]
+    loads += [(b, j, j + 4) for b in range(1, NB) for j in (0, 4)]
+    stores = [(b, j, j + 4) for b in range(NB - 1) for j in (0, 4)]
+    stores += [(NB - 1, 0, 2), (NB - 1, 2, 4), (NB - 1, 4, 6), (NB - 1, 6, 7), (NB - 1, 7, 8)]
+    load_of = {}
+    for li, (b, j0, j1) in enumerate(loads):
+        for j in range(j0, j1):
+            load_of[b * JB + j] = li
+    store_of = {}
+    for si, (b, j0, j1) in enumerate(stores):
+        for j in range(j0, j1):
+            store_of[b * JB + j] = si
+
+    with ExitStack() as ctx:
+        const = ctx.enter_context(tc.tile_pool(name="const", bufs=1))
+        xsp = ctx.enter_context(tc.tile_pool(name="xsp", bufs=8))
+        grp = ctx.enter_context(tc.tile_pool(name="grp", bufs=3))
+        cdp = ctx.enter_context(tc.tile_pool(name="cdp", bufs=3))
+        jkp = ctx.enter_context(tc.tile_pool(name="jkp", bufs=2))
+        osp = ctx.enter_context(tc.tile_pool(name="osp", bufs=4))
+        ps_t = ctx.enter_context(tc.psum_pool(name="ps_t", bufs=4))
+        ps_a = ctx.enter_context(tc.psum_pool(name="ps_a", bufs=2))
+        ps_b = ctx.enter_context(tc.psum_pool(name="ps_b", bufs=2))
+        ctx.enter_context(tc.manual_schedule())
+
+        idf = const.tile([P, P], F32, name="idf")
+        gt = const.tile([P, 4 * P], BF16, name="gt")
+        g32 = const.tile([P, 8], F32, name="g32")
+        epst = const.tile([P, 1], F32, name="epst")
+        warm = const.tile([P, 1], F32, name="warm")
+        wsb = const.tile([P, 6, D], BF16, name="wsb")
+        wg = const.tile([P, 2, NOUT, 2], F32, name="wg", align_bytes=64)
+        wc = const.tile([P, 2, NOUT], U32, name="wc", align_bytes=64)
+        ws = const.tile([P, 2, NOUT], U8, name="ws", align_bytes=64)
+        xt = [const.tile([P, j1 - j0, D], BF16, name="xt%d" % li) for li, (b, j0, j1) in enumerate(loads)]
+        ms = [const.tile([P, 2], F32, name="ms%d" % i) for i in range(NP)]
+        sq = [const.tile([P, 2], F32, name="sq%d" % i) for i in range(NP)]
+        rs = [const.tile([P, 2], F32, name="rs%d" % i) for i in range(NP)]
+
+        nc.vector.memset(gt[:], 0.0)
+        nc.vector.memset(epst[:], EPS)
+        make_identity(nc, idf[:])
+        nc.scalar.dma_start(out=gt[0:2, :], in_=norm1_w.rearrange("(r c) -> r c", c=4 * P))
+
+        def load_x(li):
+            b, j0, j1 = loads[li]
+            src = xf[b * L : (b + 1) * L, :].rearrange("(p j) d -> p j d", j=JB)
+            nc.sync.dma_start(out=xt[li][:], in_=src[:, j0:j1, :])
+
+        def load_w(a0, a1):
+            src = qkv_w.rearrange("(a p) k -> p a k", p=P)
+            nc.sync.dma_start(out=wsb[:, a0:a1, :], in_=src[:, a0:a1, :])
+
+        load_x(0)
+        load_x(1)
+        load_x(2)
+        load_w(0, 2)
+        load_w(2, 4)
+        load_w(4, 6)
+        for li in range(3, len(loads)):
+            load_x(li)
+
+        nc.scalar.activation(out=warm[:], in_=epst[:], func=ACT.Sqrt)
+
+        def x_of(t):
+            li = load_of[t]
+            return xt[li][:, t % JB - loads[li][1], :]
+
+        def sum_squares(t):
+            junk = jkp.tile([P, D], BF16, name="junk")
+            nc.scalar.activation(
+                out=junk[:], in_=x_of(t), func=ACT.Square, scale=1.0 / 32.0, accum_out=ms[t // 2][:, t % 2 : t % 2 + 1]
+            )
+
+        def root(t0, t1):
+            i = t0 // 2
+            nc.scalar.activation(
+                out=sq[i][:, t0 % 2 : t1 - 2 * i], in_=ms[i][:, t0 % 2 : t1 - 2 * i], func=ACT.Sqrt, bias=epst[:, 0:1]
+            )
+
+        def invert(t0, t1):
+            i = t0 // 2
+            nc.vector.reciprocal(out=rs[i][:, t0 % 2 : t1 - 2 * i], in_=sq[i][:, t0 % 2 : t1 - 2 * i])
+
+        xs_of = {}
+        tb_of = {}
+        gr_of = {}
+        cd_of = {}
+        o_of = {}
+        os_of = {}
+
+        def scale_rows(t, engine):
+            xs = xsp.tile([P, D], F32, name="xs")
+            xs_of[t] = xs
+            r = rs[t // 2][:, t % 2 : t % 2 + 1]
+            src = x_of(t).rearrange("q (g p u) -> q g u p", g=2, u=4)
+            dst = xs[:].rearrange("q (g u p) -> q g u p", g=2, u=4)
+            if engine == "g":
+                nc.gpsimd.tensor_scalar(out=dst, in0=src, scalar1=r, scalar2=1.0, op0=ALU.mult, op1=ALU.mult)
+            else:
+                nc.vector.tensor_scalar(out=dst, in0=src, scalar1=r, scalar2=None, op0=ALU.mult)
+
+        def transposes(t):
+            xs = xs_of[t]
+            banks = []
+            for g in range(2):
+                tb = ps_t.tile([P, 4, P], F32, name="tb")
+                for u in range(4):
+                    c = 4 * g + u
+                    nc.tensor.transpose(out=tb[:, u, :], in_=xs[:, c * P : (c + 1) * P], identity=idf[:])
+                banks.append(tb)
+            tb_of[t] = banks
+
+        def gain_and_group(t, g):
+            if t % 2 == 0 and g == 0:
+                gr_of[t // 2] = grp.tile([P, 4, P, 4], BF16, name="gr", align_bytes=64)
+            nc.vector.tensor_tensor(
+                out=gr_of[t // 2][:, 2 * (t % 2) + g, :, :],
+                in0=tb_of[t][g][:].rearrange("p u r -> p r u"),
+                in1=g32[:, 4 * g : 4 * g + 4].unsqueeze(1).to_broadcast([P, P, 4]),
+                op=ALU.mult,
+            )
+
+        def quantise(i, s0, s1):
+            if s0 == 0:
+                cd = cdp.tile([P, 4, P], U32, name="cd", align_bytes=64)
+                sc = cdp.tile([P, 4, P], U8, name="sc", align_bytes=64)
+                cd_of[i] = (cd, sc)
+            cd, sc = cd_of[i]
+            nc.vector.quantize_mx(
+                out=cd[:, s0:s1, :].rearrange("p s r -> p (s r)").bitcast(FP8X4),
+                scales=sc[:, s0:s1, :].rearrange("p s r -> p (s r)"),
+                in_=gr_of[i][:, s0:s1, :, :].rearrange("p s r u -> p (s r u)"),
+            )
+
+        def project(t):
+            cd, sc = cd_of[t // 2]
+            oa = ps_a.tile([P, 512], F32, name="oa")
+            ob = ps_b.tile([P, 256], F32, name="ob")
+            o_of[t] = (oa, ob)
+            for o, n0, n1 in ((oa, 0, 512), (ob, 512, NOUT)):
+                for g in range(2):
+                    s = 2 * (t % 2) + g
+                    nc.tensor.matmul_mx(
+                        out=o[:],
+                        lhsT=cd[:, s, :].bitcast(FP8X4),
+                        lhsT_scale=sc[:, s, :],
+                        rhs=wc[:, g, n0:n1].bitcast(FP8X4),
+                        rhs_scale=ws[:, g, n0:n1],
+                        start=(g == 0),
+                        stop=(g == 1),
+                    )
+
+        def results_out(t, engine_b):
+            si = store_of[t]
+            b, j0, j1 = stores[si]
+            j = t % JB
+            if j == j0:
+                os_of[si] = osp.tile([P, 6, j1 - j0, P], F32, name="osb")
+            osb = os_of[si]
+            oa, ob = o_of[t]
+            nc.scalar.copy(out=osb[:, 0:4, j - j0, :], in_=oa[:].rearrange("p (c f) -> p c f", c=4))
+            if engine_b == "v":
+                nc.vector.tensor_copy(out=osb[:, 4:6, j - j0, :], in_=ob[:].rearrange("p (c f) -> p c f", c=2))
+            else:
+                nc.scalar.copy(out=osb[:, 4:6, j - j0, :], in_=ob[:].rearrange("p (c f) -> p c f", c=2))
+            if j == j1 - 1:
+                for i in range(3):
+                    dst = outs[i].rearrange("b n l f -> (b n) l f")[2 * b : 2 * b + 2, :, :]
+                    dst = dst.rearrange("n (p j) f -> p n j f", j=JB)
+                    nc.sync.dma_start(out=dst[:, :, j0:j1, :], in_=osb[:, 2 * i : 2 * i + 2, :, :])
+
+        wp_of = {}
+
+        def w_transposes(a):
+            pool = ps_a if a % 4 < 2 else ps_b
+            wp = pool.tile([P, 4, P], F32, name="wp", tag="oa" if a % 4 < 2 else "ob")
+            wp_of[a] = wp
+            words = wsb[:, a, :].bitcast(F32)
+            for c in range(4):
+                g, u = c // 2, c % 2
+                nc.tensor.transpose(out=wp[:, c, :], in_=words[:, 256 * g + u : 256 * (g + 1) : 2], identity=idf[:])
+
+        def w_group(a, engine):
+            dst = wg[:, :, a * P : (a + 1) * P, :]
+            src = wp_of[a][:].rearrange("p (g u) n -> p g n u", g=2)
+            if engine == "v":
+                nc.vector.tensor_copy(out=dst, in_=src)
+            else:
+                nc.scalar.copy(out=dst, in_=src)
+
+        def w_quantise(n0, n1):
+            for g in range(2):
+                nc.vector.quantize_mx(
+                    out=wc[:, g, n0:n1].bitcast(FP8X4),
+                    scales=ws[:, g, n0:n1],
+                    in_=wg[:, g, n0:n1, :].rearrange("p n u -> p (n u)").bitcast(BF16),
+                )
+
+        def gain_columns():
+            gp = ps_t.tile([P, 2, P], F32, name="gp", tag="tb")
+            words = gt[:].bitcast(F32)
+            for u in range(2):
+                nc.tensor.transpose(out=gp[:, u, :], in_=words[:, u : 256 : 2], identity=idf[:])
+            nc.vector.tensor_copy(
+                out=g32[:].rearrange("p (g u e) -> p u g e", g=2, u=2),
+                in_=gp[:].bitcast(BF16)[:, :, 0:4].rearrange("p u (g e) -> p u g e", g=2),
+            )
+
+        sum_squares(0)
+        root(0, 1)
+        invert(0, 1)
+        gain_columns()
+        scale_rows(0, "v")
+        transposes(0)
+        sum_squares(1)
+        root(1, 2)
+        invert(1, 2)
+        scale_rows(1, "v")
+        transposes(1)
+        sum_squares(2)
+        sum_squares(3)
+        root(2, 4)
+        w_transposes(0)
+        w_transposes(1)
+        for t in range(2):
+            for g in range(2):
+                gain_and_group(t, g)
+        invert(2, 4)
+        scale_rows(2, "g")
+        scale_rows(3, "g")
+        w_group(0, "s")
+        w_group(1, "v")
+        w_transposes(2)
+        w_transposes(3)
+        w_group(2, "s")
+        w_group(3, "v")
+        w_transposes(4)
+        w_transposes(5)
+        w_group(4, "s")
+        w_group(5, "v")
+        w_quantise(0, 512)
+        w_quantise(512, NOUT)
+
+        for i in range(-1, NP):
+            a, b = 2 * i, 2 * i + 1
+            last = i == NP - 1
+            m = i - 1
+            ahead = i + PA
+            if 0 <= m < NP - 1:
+                project(2 * m)
+                project(2 * m + 1)
+            if 2 <= ahead < NP:
+                sum_squares(2 * ahead)
+            if 1 <= i < NP:
+                gain_and_group(a, 0)
+                gain_and_group(a, 1)
+                gain_and_group(b, 0)
+                if not last:
+                    gain_and_group(b, 1)
+            if 0 <= m < NP - 1:
+                results_out(2 * m, "v" if 2 * m < FB_V_UNTIL else "s")
+            if 2 <= ahead < NP:
+                sum_squares(2 * ahead + 1)
+            if 0 <= m < NP - 1:
+                results_out(2 * m + 1, "v" if 2 * m < FB_V_UNTIL else "s")
+            if 2 <= ahead < NP:
+                root(2 * ahead, 2 * ahead + 2)
+            if last:
+                quantise(i, 0, 2)
+                project(a)
+                gain_and_group(b, 1)
+                quantise(i, 2, 4)
+                project(b)
+                results_out(a, "s")
+                results_out(b, "v")
+            if 2 <= i + PI < NP:
+                invert(2 * (i + PI), 2 * (i + PI) + 2)
+                scale_rows(2 * (i + PI), "g")
+                scale_rows(2 * (i + PI) + 1, "g")
+            if 0 <= i < NP - 1:
+                quantise(i, 0, 4)
+            if 0 <= i < NP - 1:
+                transposes(a + 2)
+                transposes(b + 2)

@@ -58,8 +58,7 @@ def tile_transformerblock_pa_t_kernel(tc, x, norm1_w, qkv_w, out_0, out_1, out_2
         ctx.enter_context(tc.manual_schedule())
 
         idf = const.tile([P, P], F32, name="idf")
-        gt = const.tile([P, 4 * P], BF16, name="gt")
-        g32 = const.tile([P, 8], F32, name="g32")
+        gn = const.tile([P, 2, 4], BF16, name="gn")
         epst = const.tile([P, 1], F32, name="epst")
         warm = const.tile([P, 1], F32, name="warm")
         wsb = const.tile([P, 6, D], BF16, name="wsb")
@@ -71,10 +70,9 @@ def tile_transformerblock_pa_t_kernel(tc, x, norm1_w, qkv_w, out_0, out_1, out_2
         sq = [const.tile([P, 2], F32, name="sq%d" % i) for i in range(NP)]
         rs = [const.tile([P, 2], F32, name="rs%d" % i) for i in range(NP)]
 
-        nc.vector.memset(gt[:], 0.0)
         nc.vector.memset(epst[:], EPS)
         make_identity(nc, idf[:])
-        nc.scalar.dma_start(out=gt[0:2, :], in_=norm1_w.rearrange("(r c) -> r c", c=4 * P))
+        nc.scalar.dma_start(out=gn[:], in_=norm1_w.rearrange("(g p u) -> p g u", g=2, u=4))
 
         def load_x(li):
             b, j0, j1 = loads[li]
@@ -151,7 +149,7 @@ def tile_transformerblock_pa_t_kernel(tc, x, norm1_w, qkv_w, out_0, out_1, out_2
             nc.vector.tensor_tensor(
                 out=gr_of[t // 2][:, 2 * (t % 2) + g, :, :],
                 in0=tb_of[t][g][:].rearrange("p u r -> p r u"),
-                in1=g32[:, 4 * g : 4 * g + 4].unsqueeze(1).to_broadcast([P, P, 4]),
+                in1=gn[:, g, :].unsqueeze(1).to_broadcast([P, P, 4]),
                 op=ALU.mult,
             )
 
@@ -231,20 +229,9 @@ def tile_transformerblock_pa_t_kernel(tc, x, norm1_w, qkv_w, out_0, out_1, out_2
                     in_=wg[:, g, n0:n1, :].rearrange("p n u -> p (n u)").bitcast(BF16),
                 )
 
-        def gain_columns():
-            gp = ps_t.tile([P, 2, P], F32, name="gp", tag="tb")
-            words = gt[:].bitcast(F32)
-            for u in range(2):
-                nc.tensor.transpose(out=gp[:, u, :], in_=words[:, u : 256 : 2], identity=idf[:])
-            nc.vector.tensor_copy(
-                out=g32[:].rearrange("p (g u e) -> p u g e", g=2, u=2),
-                in_=gp[:].bitcast(BF16)[:, :, 0:4].rearrange("p u (g e) -> p u g e", g=2),
-            )
-
         sum_squares(0)
         root(0, 1)
         invert(0, 1)
-        gain_columns()
         scale_rows(0, "v")
         transposes(0)
         sum_squares(1)

@@ -22,6 +22,7 @@ NP = NT // 2
 EPS = 1e-6
 FLOPS = 2 * NB * L * D * NOUT
 
+SS = 29
 PA = 3
 PI = 2
 FB_V_UNTIL = 24
@@ -104,6 +105,13 @@ def tile_transformerblock_pa_t_kernel(tc, x, norm1_w, qkv_w, out_0, out_1, out_2
                 out=junk[:], in_=x_of(t), func=ACT.Square, scale=1.0 / 32.0, accum_out=ms[t // 2][:, t % 2 : t % 2 + 1]
             )
 
+        def sum_squares_v(t):
+            junk = jkp.tile([P, D], BF16, name="junkv")
+            nc.vector.scalar_tensor_tensor(
+                out=junk[:], in0=x_of(t), scalar=1.0 / D, in1=x_of(t), op0=ALU.mult, op1=ALU.mult,
+                accum_out=ms[t // 2][:, t % 2 : t % 2 + 1],
+            )
+
         def root(t0, t1):
             i = t0 // 2
             nc.scalar.activation(
@@ -127,7 +135,9 @@ def tile_transformerblock_pa_t_kernel(tc, x, norm1_w, qkv_w, out_0, out_1, out_2
             r = rs[t // 2][:, t % 2 : t % 2 + 1]
             src = x_of(t).rearrange("q (g p u) -> q g u p", g=2, u=4)
             dst = xs[:].rearrange("q (g u p) -> q g u p", g=2, u=4)
-            if engine == "g":
+            if engine == "s":
+                nc.scalar.activation(out=dst, in_=src, func=ACT.Copy, scale=r)
+            elif engine == "g":
                 nc.gpsimd.tensor_scalar(out=dst, in0=src, scalar1=r, scalar2=1.0, op0=ALU.mult, op1=ALU.mult)
             else:
                 nc.vector.tensor_scalar(out=dst, in0=src, scalar1=r, scalar2=None, op0=ALU.mult)
@@ -230,26 +240,27 @@ def tile_transformerblock_pa_t_kernel(tc, x, norm1_w, qkv_w, out_0, out_1, out_2
                 )
 
         sum_squares(0)
+        sum_squares_v(1)
         root(0, 1)
         invert(0, 1)
         scale_rows(0, "v")
         transposes(0)
-        sum_squares(1)
+        sum_squares(2)
         root(1, 2)
         invert(1, 2)
         scale_rows(1, "v")
         transposes(1)
-        sum_squares(2)
         sum_squares(3)
         root(2, 4)
         w_transposes(0)
         w_transposes(1)
-        for t in range(2):
-            for g in range(2):
-                gain_and_group(t, g)
+        gain_and_group(0, 0)
+        gain_and_group(0, 1)
         invert(2, 4)
         scale_rows(2, "g")
         scale_rows(3, "g")
+        gain_and_group(1, 0)
+        gain_and_group(1, 1)
         w_group(0, "s")
         w_group(1, "v")
         w_transposes(2)
@@ -297,8 +308,8 @@ def tile_transformerblock_pa_t_kernel(tc, x, norm1_w, qkv_w, out_0, out_1, out_2
                 results_out(b, "v")
             if 2 <= i + PI < NP:
                 invert(2 * (i + PI), 2 * (i + PI) + 2)
-                scale_rows(2 * (i + PI), "g")
-                scale_rows(2 * (i + PI) + 1, "g")
+                scale_rows(2 * (i + PI), "s" if 2 * (i + PI) >= SS else "g")
+                scale_rows(2 * (i + PI) + 1, "s" if 2 * (i + PI) + 1 >= SS else "g")
             if 0 <= i < NP - 1:
                 quantise(i, 0, 4)
             if 0 <= i < NP - 1:

@@ -245,6 +245,7 @@ def tile_transformerblock_pa_t_kernel(tc, x, norm1_w, qkv_w, out_0, out_1, out_2
         invert(0, 1)
         scale_rows(0, "v")
         transposes(0)
+        w_transposes(0)
         sum_squares(2)
         root(1, 2)
         invert(1, 2)
@@ -252,7 +253,6 @@ def tile_transformerblock_pa_t_kernel(tc, x, norm1_w, qkv_w, out_0, out_1, out_2
         transposes(1)
         sum_squares(3)
         root(2, 4)
-        w_transposes(0)
         w_transposes(1)
         gain_and_group(0, 0)
         gain_and_group(0, 1)

from contextlib import ExitStack

import concourse.mybir as mybir
from concourse.masks import make_identity

BF16 = mybir.dt.bfloat16
F32 = mybir.dt.float32
U32 = mybir.dt.uint32
U8 = mybir.dt.uint8
FP8X4 = mybir.dt.float8_e4m3fn_x4
ACT = mybir.ActivationFunctionType
ALU = mybir.AluOpType

P = 128
NB = 4
L = 1024
D = 1024
NOUT = 768
JB = L // P
NT = NB * JB
NP = NT // 2
EPS = 1e-6
FLOPS = 2 * NB * L * D * NOUT

SS = 29
PA = 3
PI = 2
FB_V_UNTIL = 24


def tile_transformerblock_pa_t_kernel(tc, x, norm1_w, qkv_w, out_0, out_1, out_2):
    nc = tc.nc
    outs = (out_0, out_1, out_2)
    xf = x.flatten_outer_dims()

    loads = [(0, 0, 1), (0, 1, 2), (0, 2, 4), (0, 4, 8)]
    loads += [(b, j, j + 4) for b in range(1, NB) for j in (0, 4)]
    stores = [(b, j, j + 4) for b in range(NB - 1) for j in (0, 4)]
    stores += [(NB - 1, 0, 2), (NB - 1, 2, 4), (NB - 1, 4, 6), (NB - 1, 6, 7), (NB - 1, 7, 8)]
    load_of = {}
    for li, (b, j0, j1) in enumerate(loads):
        for j in range(j0, j1):
            load_of[b * JB + j] = li
    store_of = {}
    for si, (b, j0, j1) in enumerate(stores):
        for j in range(j0, j1):
            store_of[b * JB + j] = si

    with ExitStack() as ctx:
        const = ctx.enter_context(tc.tile_pool(name="const", bufs=1))
        xsp = ctx.enter_context(tc.tile_pool(name="xsp", bufs=8))
        grp = ctx.enter_context(tc.tile_pool(name="grp", bufs=3))
        cdp = ctx.enter_context(tc.tile_pool(name="cdp", bufs=3))
        jkp = ctx.enter_context(tc.tile_pool(name="jkp", bufs=2))
        osp = ctx.enter_context(tc.tile_pool(name="osp", bufs=4))
        ps_t = ctx.enter_context(tc.psum_pool(name="ps_t", bufs=4))
        ps_a = ctx.enter_context(tc.psum_pool(name="ps_a", bufs=2))
        ps_b = ctx.enter_context(tc.psum_pool(name="ps_b", bufs=2))
        ctx.enter_context(tc.manual_schedule())

        idf = const.tile([P, P], F32, name="idf")
        gn = const.tile([P, 2, 4], BF16, name="gn")
        epst = const.tile([P, 1], F32, name="epst")
        warm = const.tile([P, 1], F32, name="warm")
        wsb = const.tile([P, 6, D], BF16, name="wsb")
        wg = const.tile([P, 2, NOUT, 2], F32, name="wg", align_bytes=64)
        wc = const.tile([P, 2, NOUT], U32, name="wc", align_bytes=64)
        ws = const.tile([P, 2, NOUT], U8, name="ws", align_bytes=64)
        xt = [const.tile([P, j1 - j0, D], BF16, name="xt%d" % li) for li, (b, j0, j1) in enumerate(loads)]
        ms = [const.tile([P, 2], F32, name="ms%d" % i) for i in range(NP)]
        sq = [const.tile([P, 2], F32, name="sq%d" % i) for i in range(NP)]
        rs = [const.tile([P, 2], F32, name="rs%d" % i) for i in range(NP)]

        nc.vector.memset(epst[:], EPS)
        make_identity(nc, idf[:])
        nc.scalar.dma_start(out=gn[:], in_=norm1_w.rearrange("(g p u) -> p g u", g=2, u=4))

        def load_x(li):
            b, j0, j1 = loads[li]
            src = xf[b * L : (b + 1) * L, :].rearrange("(p j) d -> p j d", j=JB)
            nc.sync.dma_start(out=xt[li][:], in_=src[:, j0:j1, :])

        def load_w(a0, a1):
            src = qkv_w.rearrange("(a p) k -> p a k", p=P)
            nc.sync.dma_start(out=wsb[:, a0:a1, :], in_=src[:, a0:a1, :])

        load_x(0)
        load_x(1)
        load_x(2)
        load_w(0, 2)
        load_w(2, 4)
        load_w(4, 6)
        for li in range(3, len(loads)):
            load_x(li)

        nc.scalar.activation(out=warm[:], in_=epst[:], func=ACT.Sqrt)

        def x_of(t):
            li = load_of[t]
            return xt[li][:, t % JB - loads[li][1], :]

        def sum_squares(t):
            junk = jkp.tile([P, D], BF16, name="junk")
            nc.scalar.activation(
                out=junk[:], in_=x_of(t), func=ACT.Square, scale=1.0 / 32.0, accum_out=ms[t // 2][:, t % 2 : t % 2 + 1]
            )

        def sum_squares_v(t):
            junk = jkp.tile([P, D], BF16, name="junkv")
            nc.vector.scalar_tensor_tensor(
                out=junk[:], in0=x_of(t), scalar=1.0 / D, in1=x_of(t), op0=ALU.mult, op1=ALU.mult,
                accum_out=ms[t // 2][:, t % 2 : t % 2 + 1],
            )

        def root(t0, t1):
            i = t0 // 2
            nc.scalar.activation(
                out=sq[i][:, t0 % 2 : t1 - 2 * i], in_=ms[i][:, t0 % 2 : t1 - 2 * i], func=ACT.Sqrt, bias=epst[:, 0:1]
            )

        def invert(t0, t1):
            i = t0 // 2
            nc.vector.reciprocal(out=rs[i][:, t0 % 2 : t1 - 2 * i], in_=sq[i][:, t0 % 2 : t1 - 2 * i])

        xs_of = {}
        tb_of = {}
        gr_of = {}
        cd_of = {}
        o_of = {}
        os_of = {}

        def scale_rows(t, engine):
            xs = xsp.tile([P, D], F32, name="xs")
            xs_of[t] = xs
            r = rs[t // 2][:, t % 2 : t % 2 + 1]
            src = x_of(t).rearrange("q (g p u) -> q g u p", g=2, u=4)
            dst = xs[:].rearrange("q (g u p) -> q g u p", g=2, u=4)
            if engine == "s":
                nc.scalar.activation(out=dst, in_=src, func=ACT.Copy, scale=r)
            elif engine == "g":
                nc.gpsimd.tensor_scalar(out=dst, in0=src, scalar1=r, scalar2=1.0, op0=ALU.mult, op1=ALU.mult)
            else:
                nc.vector.tensor_scalar(out=dst, in0=src, scalar1=r, scalar2=None, op0=ALU.mult)

        def transposes(t):
            xs = xs_of[t]
            banks = []
            for g in range(2):
                tb = ps_t.tile([P, 4, P], F32, name="tb")
                for u in range(4):
                    c = 4 * g + u
                    nc.tensor.transpose(out=tb[:, u, :], in_=xs[:, c * P : (c + 1) * P], identity=idf[:])
                banks.append(tb)
            tb_of[t] = banks

        def gain_and_group(t, g):
            if t % 2 == 0 and g == 0:
                gr_of[t // 2] = grp.tile([P, 4, P, 4], BF16, name="gr", align_bytes=64)
            nc.vector.tensor_tensor(
                out=gr_of[t // 2][:, 2 * (t % 2) + g, :, :],
                in0=tb_of[t][g][:].rearrange("p u r -> p r u"),
                in1=gn[:, g, :].unsqueeze(1).to_broadcast([P, P, 4]),
                op=ALU.mult,
            )

        def quantise(i, s0, s1):
            if s0 == 0:
                cd = cdp.tile([P, 4, P], U32, name="cd", align_bytes=64)
                sc = cdp.tile([P, 4, P], U8, name="sc", align_bytes=64)
                cd_of[i] = (cd, sc)
            cd, sc = cd_of[i]
            nc.vector.quantize_mx(
                out=cd[:, s0:s1, :].rearrange("p s r -> p (s r)").bitcast(FP8X4),
                scales=sc[:, s0:s1, :].rearrange("p s r -> p (s r)"),
                in_=gr_of[i][:, s0:s1, :, :].rearrange("p s r u -> p (s r u)"),
            )

        def project(t):
            cd, sc = cd_of[t // 2]
            oa = ps_a.tile([P, 512], F32, name="oa")
            ob = ps_b.tile([P, 256], F32, name="ob")
            o_of[t] = (oa, ob)
            for o, n0, n1 in ((oa, 0, 512), (ob, 512, NOUT)):
                for g in range(2):
                    s = 2 * (t % 2) + g
                    nc.tensor.matmul_mx(
                        out=o[:],
                        lhsT=cd[:, s, :].bitcast(FP8X4),
                        lhsT_scale=sc[:, s, :],
                        rhs=wc[:, g, n0:n1].bitcast(FP8X4),
                        rhs_scale=ws[:, g, n0:n1],
                        start=(g == 0),
                        stop=(g == 1),
                    )

        def results_out(t, engine_b):
            si = store_of[t]
            b, j0, j1 = stores[si]
            j = t % JB
            if j == j0:
                os_of[si] = osp.tile([P, 6, j1 - j0, P], F32, name="osb")
            osb = os_of[si]
            oa, ob = o_of[t]
            nc.scalar.copy(out=osb[:, 0:4, j - j0, :], in_=oa[:].rearrange("p (c f) -> p c f", c=4))
            if engine_b == "v":
                nc.vector.tensor_copy(out=osb[:, 4:6, j - j0, :], in_=ob[:].rearrange("p (c f) -> p c f", c=2))
            else:
                nc.scalar.copy(out=osb[:, 4:6, j - j0, :], in_=ob[:].rearrange("p (c f) -> p c f", c=2))
            if j == j1 - 1:
                for i in range(3):
                    dst = outs[i].rearrange("b n l f -> (b n) l f")[2 * b : 2 * b + 2, :, :]
                    dst = dst.rearrange("n (p j) f -> p n j f", j=JB)
                    nc.sync.dma_start(out=dst[:, :, j0:j1, :], in_=osb[:, 2 * i : 2 * i + 2, :, :])

        wp_of = {}

        def w_transposes(a):
            pool = ps_a if a % 4 < 2 else ps_b
            wp = pool.tile([P, 4, P], F32, name="wp", tag="oa" if a % 4 < 2 else "ob")
            wp_of[a] = wp
            words = wsb[:, a, :].bitcast(F32)
            for c in range(4):
                g, u = c // 2, c % 2
                nc.tensor.transpose(out=wp[:, c, :], in_=words[:, 256 * g + u : 256 * (g + 1) : 2], identity=idf[:])

        def w_group(a, engine):
            dst = wg[:, :, a * P : (a + 1) * P, :]
            src = wp_of[a][:].rearrange("p (g u) n -> p g n u", g=2)
            if engine == "v":
                nc.vector.tensor_copy(out=dst, in_=src)
            else:
                nc.scalar.copy(out=dst, in_=src)

        def w_quantise(n0, n1):
            for g in range(2):
                nc.vector.quantize_mx(
                    out=wc[:, g, n0:n1].bitcast(FP8X4),
                    scales=ws[:, g, n0:n1],
                    in_=wg[:, g, n0:n1, :].rearrange("p n u -> p (n u)").bitcast(BF16),
                )

        sum_squares(0)
        sum_squares_v(1)
        root(0, 1)
        invert(0, 1)
        scale_rows(0, "v")
        transposes(0)
        w_transposes(0)
        sum_squares(2)
        root(1, 2)
        invert(1, 2)
        scale_rows(1, "v")
        transposes(1)
        sum_squares(3)
        root(2, 4)
        w_transposes(1)
        gain_and_group(0, 0)
        gain_and_group(0, 1)
        invert(2, 4)
        scale_rows(2, "g")
        scale_rows(3, "g")
        gain_and_group(1, 0)
        gain_and_group(1, 1)
        w_group(0, "s")
        w_group(1, "v")
        w_transposes(2)
        w_transposes(3)
        w_group(2, "s")
        w_group(3, "v")
        w_transposes(4)
        w_transposes(5)
        w_group(4, "s")
        w_group(5, "v")
        w_quantise(0, 512)
        w_quantise(512, NOUT)

        for i in range(-1, NP):
            a, b = 2 * i, 2 * i + 1
            last = i == NP - 1
            m = i - 1
            ahead = i + PA
            if 0 <= m < NP - 1:
                project(2 * m)
                project(2 * m + 1)
            if 2 <= ahead < NP:
                sum_squares(2 * ahead)
            if 1 <= i < NP:
                gain_and_group(a, 0)
                gain_and_group(a, 1)
                gain_and_group(b, 0)
                if not last:
                    gain_and_group(b, 1)
            if 0 <= m < NP - 1:
                results_out(2 * m, "v" if 2 * m < FB_V_UNTIL else "s")
            if 2 <= ahead < NP:
                sum_squares(2 * ahead + 1)
            if 0 <= m < NP - 1:
                results_out(2 * m + 1, "v" if 2 * m < FB_V_UNTIL else "s")
            if 2 <= ahead < NP:
                root(2 * ahead, 2 * ahead + 2)
            if last:
                quantise(i, 0, 2)
                project(a)
                gain_and_group(b, 1)
                quantise(i, 2, 4)
                project(b)
                results_out(a, "s")
                results_out(b, "v")
            if 2 <= i + PI < NP:
                invert(2 * (i + PI), 2 * (i + PI) + 2)
                scale_rows(2 * (i + PI), "s" if 2 * (i + PI) >= SS else "g")
                scale_rows(2 * (i + PI) + 1, "s" if 2 * (i + PI) + 1 >= SS else "g")
            if 0 <= i < NP - 1:
                quantise(i, 0, 4)
            if 0 <= i < NP - 1:
                transposes(a + 2)
                transposes(b + 2)
